import numpy as np
import ml_dtypes


def mxq(x, axis, fmt="e4m3"):
    dtype, down = {"e4m3": (ml_dtypes.float8_e4m3fn, 7), "e5m2": (ml_dtypes.float8_e5m2, 14)}[fmt]
    v = np.moveaxis(np.asarray(x, np.float32).astype(ml_dtypes.bfloat16).astype(np.float64), axis, -1)
    blocks = v.reshape(v.shape[:-1] + (-1, 32))
    amax = np.abs(blocks).max(-1, keepdims=True)
    byte = np.maximum(np.where(amax > 0, np.frexp(amax)[1] - 1 + 127, 0) - down, 1)
    scale = np.exp2(byte - 127.0)
    codes = (blocks / scale).astype(np.float32).astype(dtype).astype(np.float64)
    return np.moveaxis((codes * scale).reshape(v.shape), -1, axis)


WIDE = False


def mx_kscale(k):
    if not WIDE:
        return np.ones(k)
    levels = np.array([10, -10, 5, -5, 0])
    a = np.random.permutation(np.resize(levels, k // 512 * 4)).reshape(k // 512, 4)
    idx = np.arange(k)
    return np.exp2(a[idx // 512, idx % 128 // 32])


BF16 = ml_dtypes.bfloat16


def bf(x):
    return np.asarray(x, np.float32).astype(BF16)


def f64(x):
    return np.asarray(x).astype(np.float64)


E2M1 = np.array([0.0, 0.5, 1.0, 1.5, 2.0, 3.0, 4.0, 6.0, -0.0, -0.5, -1.0, -1.5, -2.0, -3.0, -4.0, -6.0])


def pack_weight(w, fmt):
    k, n = w.shape
    w = f64(bf(w)).reshape(k // 32, 32, n)
    amax = np.abs(w).max(1)
    if fmt == "e4m3":
        byte = np.frexp(amax)[1] - 1 + 127 - 7
    else:
        mant, ex = np.frexp(amax / 6.0)
        byte = np.where(mant > 0.5, ex, ex - 1) + 127
    byte = np.clip(np.where(amax > 0, byte, 1), 1, 254)
    scaled = (w * np.exp2(127.0 - byte)[:, None, :]).reshape(k, n).astype(np.float32)
    by_word = np.ascontiguousarray(scaled.reshape(k // 512, 128, 4, n).transpose(0, 1, 3, 2))
    if fmt == "e4m3":
        words = by_word.astype(ml_dtypes.float8_e4m3fn).view(np.uint8)
    else:
        c = by_word.astype(ml_dtypes.float4_e2m1fn).view(np.uint8) & 0xF
        words = c[..., 0::2] | (c[..., 1::2] << 4)
    return np.ascontiguousarray(words), np.ascontiguousarray(byte.astype(np.uint8).reshape(k // 512, 16, n))


def unpack_weight(words, scales, fmt):
    g, p, n, _ = words.shape
    if fmt == "e4m3":
        vals = np.ascontiguousarray(words).view(ml_dtypes.float8_e4m3fn).astype(np.float64)
    else:
        nib = np.empty((g, p, n, 4), np.uint8)
        nib[..., 0::2] = words & 0xF
        nib[..., 1::2] = words >> 4
        vals = E2M1[nib]
    vals = vals * np.repeat(np.exp2(scales.astype(np.float64) - 127.0), 8, axis=1)[..., None]
    return vals.transpose(0, 1, 3, 2).reshape(g * 512, n)

def pack4(w):
    words, scales = pack_weight(w, "e2m1")
    return words.reshape(words.shape[0], 128, -1), scales


def unpack4(words, scales):
    return unpack_weight(words.reshape(words.shape[0], 128, -1, 2), scales, "e2m1")


B, S, D, H, DH = 4, 2048, 1024, 1, 64
ROPE_BASE = 10000.0


def rope_tables():
    inv_freq = 1.0 / (ROPE_BASE ** (f64(np.arange(0, DH, 2)) / DH))
    freqs = f64(np.arange(S))[:, None] * inv_freq[None, :]
    return np.cos(freqs), np.sin(freqs)


def rope_interleaved(t, cos, sin):
    x1 = t[..., 0::2]
    x2 = t[..., 1::2]
    c = cos[None, :, None, :]
    s_ = sin[None, :, None, :]
    even = x1 * c - x2 * s_
    odd = x1 * s_ + x2 * c
    return np.stack((even, odd), axis=-1).reshape(t.shape)


def setup_inputs():
    s = mx_kscale(D)
    x = bf(np.random.standard_normal((B, S, D)) * s)
    w = np.random.standard_normal((2 * H * DH, D)) / np.sqrt(D) / s[None, :]
    words, scales = pack4(np.ascontiguousarray(w.T))
    return {"x": x, "wqk_w_words": words, "wqk_w_scales": scales}


def reference(x, wqk_w_words, wqk_w_scales):
    xqk = (mxq(f64(x), 2, "e4m3") @ unpack4(wqk_w_words, wqk_w_scales)).reshape(B, S, 2, H, DH)
    cos, sin = rope_tables()
    q = rope_interleaved(xqk[:, :, 0], cos, sin).transpose(0, 2, 1, 3)
    k = rope_interleaved(xqk[:, :, 1], cos, sin).transpose(0, 2, 1, 3)
    return q, k

@@ -1,0 +1,224 @@
+import math
+from contextlib import ExitStack
+
+import concourse.mybir as mybir
+from concourse.masks import make_identity
+
+F32 = mybir.dt.float32
+BF16 = mybir.dt.bfloat16
+I32 = mybir.dt.int32
+U32 = mybir.dt.uint32
+U8 = mybir.dt.uint8
+FP8X4 = mybir.dt.float8_e4m3fn_x4
+FP4X4 = mybir.dt.float4_e2m1fn_x4
+ALU = mybir.AluOpType
+ACT = mybir.ActivationFunctionType
+
+BATCH, SEQ, FEATURES = 4, 2048, 1024
+HEAD = 64
+PAIRS = HEAD // 2
+OUT_COLS = 2 * HEAD
+ROPE_BASE = 10000.0
+
+P = 128
+PACK = 4
+K_PASS = P * PACK
+PASSES = FEATURES // K_PASS
+WORDS_PER_PASS = K_PASS // 2
+
+ROWS = SEQ // P
+GROUP = 4
+GROUPS_PER_BATCH = ROWS // GROUP
+GROUPS = BATCH * GROUPS_PER_BATCH
+
+ROUND_MAGIC = 12582912.0
+
+FLOPS = 2 * BATCH * SEQ * FEATURES * OUT_COLS
+
+
+def tile_attention_pa_t_kernel(tc, x, wqk_w_words, wqk_w_scales, out_0, out_1):
+    nc = tc.nc
+    with ExitStack() as ctx:
+        ctx.enter_context(tc.manual_schedule())
+        const = ctx.enter_context(tc.tile_pool(name="const", bufs=1))
+        x_pool = ctx.enter_context(tc.tile_pool(name="x_pool", bufs=1))
+        quant = ctx.enter_context(tc.tile_pool(name="quant", bufs=2))
+        rope = ctx.enter_context(tc.tile_pool(name="rope", bufs=4))
+        xt_pool = ctx.enter_context(tc.psum_pool(name="xt_pool", bufs=6))
+        acc_pool = ctx.enter_context(tc.psum_pool(name="acc_pool", bufs=2))
+
+        x_rows = []
+        for g in range(GROUPS):
+            x_rows.append(x_pool.tile([P, GROUP, FEATURES], BF16, name="x_rows_%d" % g))
+
+        def load_x(g):
+            b, chunk = divmod(g, GROUPS_PER_BATCH)
+            rows = x[b].rearrange("(p m) k -> p m k", m=ROWS)
+            nc.sync.dma_start(out=x_rows[g][:], in_=rows[:, GROUP * chunk : GROUP * (chunk + 1), :])
+
+        w_words = const.tile([P, PASSES, 2 * OUT_COLS], U8, align_bytes=64)
+        w_scales = const.tile([P, PASSES, OUT_COLS], U8, align_bytes=64)
+        nc.vector.memset(w_scales[:].bitcast(I32), 0)
+
+        load_x(0)
+        nc.sync.dma_start(
+            out=w_words[:].bitcast(I32), in_=wqk_w_words.bitcast(I32).rearrange("c p n -> p c n")
+        )
+        scale_rows = wqk_w_scales.bitcast(I32)
+        for quadrant in range(4):
+            nc.sync.dma_start(
+                out=w_scales[32 * quadrant : 32 * quadrant + 4].bitcast(I32),
+                in_=scale_rows[:, 4 * quadrant : 4 * quadrant + 4, :].rearrange("c r n -> r c n"),
+            )
+        for g in range(1, GROUPS):
+            load_x(g)
+
+        position_int = const.tile([P, ROWS], I32)
+        nc.gpsimd.iota(position_int[:], pattern=[[1, ROWS]], base=0, channel_multiplier=ROWS)
+        ident = const.tile([P, P], F32)
+        make_identity(nc, ident[:])
+        position = const.tile([P, ROWS], F32)
+        nc.vector.tensor_copy(out=position[:], in_=position_int[:])
+        turns = const.tile([P, 2, ROWS, PAIRS], F32)
+        for i in range(PAIRS):
+            turns_per_position = ROPE_BASE ** (-2.0 * i / HEAD) / (2.0 * math.pi)
+            nc.vector.tensor_scalar(
+                out=turns[:, 0, :, i],
+                in0=position[:],
+                scalar1=turns_per_position,
+                scalar2=None,
+                op0=ALU.mult,
+            )
+        nc.vector.tensor_scalar(
+            out=turns[:, 1], in0=turns[:, 0], scalar1=0.25, scalar2=None, op0=ALU.add
+        )
+        whole_turns = const.tile([P, 2, ROWS, PAIRS], F32)
+        nc.vector.tensor_scalar(
+            out=whole_turns[:],
+            in0=turns[:],
+            scalar1=ROUND_MAGIC,
+            scalar2=ROUND_MAGIC,
+            op0=ALU.add,
+            op1=ALU.subtract,
+        )
+        part_turns = const.tile([P, 2, ROWS, PAIRS], F32)
+        nc.vector.tensor_tensor(
+            out=part_turns[:], in0=turns[:], in1=whole_turns[:], op=ALU.subtract
+        )
+        sin_cos = const.tile([P, 2, ROWS, PAIRS], F32)
+        nc.scalar.activation(out=sin_cos[:], in_=part_turns[:], func=ACT.Sin, scale=2.0 * math.pi)
+        sin = sin_cos[:, 0]
+        neg_sin = const.tile([P, ROWS, PAIRS], F32)
+        nc.vector.tensor_scalar(
+            out=neg_sin[:], in0=sin, scalar1=-1.0, scalar2=None, op0=ALU.mult
+        )
+        cos_twice = const.tile([P, ROWS, HEAD], F32)
+        nc.vector.tensor_copy(
+            out=cos_twice[:].rearrange("p m (i e) -> p (m i) e", e=2),
+            in_=sin_cos[:, 1]
+            .rearrange("p m i -> p (m i)")
+            .unsqueeze(2)
+            .to_broadcast([P, ROWS * PAIRS, 2]),
+        )
+
+        grouped_of = {}
+        codes_of = {}
+        acc_of = {}
+        rotated_of = {}
+
+        def transpose_group(g):
+            grouped = quant.tile([P, GROUP, PASSES, P, PACK], BF16, align_bytes=64)
+            grouped_of[g] = grouped
+            for j in range(GROUP):
+                words = x_rows[g][:, j, :].bitcast(F32)
+                xt = xt_pool.tile([P, PASSES, 2, P], F32)
+                for c in range(PASSES):
+                    for u in range(2):
+                        first = WORDS_PER_PASS * c + u
+                        nc.tensor.transpose(
+                            xt[:, c, u, :],
+                            words[:, first : WORDS_PER_PASS * (c + 1) : 2],
+                            ident[:],
+                        )
+                nc.scalar.copy(
+                    out=grouped[:, j].bitcast(F32), in_=xt[:].rearrange("p c u r -> p c r u")
+                )
+
+        def quantise_group(g):
+            codes = quant.tile([P, GROUP, PASSES, P], U32, align_bytes=64)
+            scales = quant.tile([P, GROUP, PASSES, P], U8, align_bytes=64)
+            codes_of[g] = (codes, scales)
+            nc.vector.quantize_mx(
+                out=codes[:].rearrange("p j c r -> p (j c r)").bitcast(FP8X4),
+                scales=scales[:].rearrange("p j c r -> p (j c r)"),
+                in_=grouped_of[g][:].rearrange("p j c r t -> p (j c r t)"),
+            )
+
+        def multiply_group(g):
+            codes, scales = codes_of[g]
+            acc = acc_pool.tile([P, GROUP, OUT_COLS], F32)
+            acc_of[g] = acc
+            for j in range(GROUP):
+                for c in range(PASSES):
+                    nc.tensor.matmul_mx(
+                        out=acc[:, j, :],
+                        lhsT=codes[:, j, c, :].bitcast(FP8X4),
+                        lhsT_scale=scales[:, j, c, :],
+                        rhs=w_words[:, c, :].bitcast(FP4X4),
+                        rhs_scale=w_scales[:, c, :],
+                        start=(c == 0),
+                        stop=(c == PASSES - 1),
+                    )
+
+        def rotation_products(g):
+            chunk = g % GROUPS_PER_BATCH
+            tiles = slice(GROUP * chunk, GROUP * (chunk + 1))
+            acc = acc_of[g]
+            pairs = acc[:].rearrange("p j (h i e) -> p j h i e", h=2, e=2)
+            rotated = rope.tile([P, 2, GROUP, HEAD], F32)
+            cross = rope.tile([P, 2, 2, GROUP, PAIRS], F32)
+            rotated_of[g] = (rotated, cross)
+            nc.vector.tensor_tensor(
+                out=cross[:, 0].rearrange("p h j i -> p j h i"),
+                in0=pairs[:, :, :, :, 1],
+                in1=neg_sin[:, tiles, :].unsqueeze(2).to_broadcast([P, GROUP, 2, PAIRS]),
+                op=ALU.mult,
+            )
+            nc.vector.tensor_tensor(
+                out=cross[:, 1].rearrange("p h j i -> p j h i"),
+                in0=pairs[:, :, :, :, 0],
+                in1=sin[:, tiles, :].unsqueeze(2).to_broadcast([P, GROUP, 2, PAIRS]),
+                op=ALU.mult,
+            )
+            nc.vector.tensor_tensor(
+                out=rotated[:].rearrange("p h j f -> p j h f"),
+                in0=acc[:].rearrange("p j (h f) -> p j h f", h=2),
+                in1=cos_twice[:, tiles, :].unsqueeze(2).to_broadcast([P, GROUP, 2, HEAD]),
+                op=ALU.mult,
+            )
+
+        def rotation_sum_and_store(g):
+            b, chunk = divmod(g, GROUPS_PER_BATCH)
+            tiles = slice(GROUP * chunk, GROUP * (chunk + 1))
+            rotated, cross = rotated_of[g]
+            by_pair = rotated[:].rearrange("p h j (i e) -> p (h j i) e", e=2)
+            nc.vector.tensor_tensor(
+                out=by_pair,
+                in0=by_pair,
+                in1=cross[:].rearrange("p e h j i -> p (h j i) e"),
+                op=ALU.add,
+            )
+            for h, out in enumerate((out_0, out_1)):
+                rows = out[b, 0].rearrange("(p m) f -> p m f", m=ROWS)
+                nc.sync.dma_start(out=rows[:, tiles, :], in_=rotated[:, h])
+
+        for step in range(GROUPS + 3):
+            if step < GROUPS:
+                transpose_group(step)
+            if 0 <= step - 1 < GROUPS:
+                quantise_group(step - 1)
+                multiply_group(step - 1)
+            if 0 <= step - 3 < GROUPS:
+                rotation_sum_and_store(step - 3)
+            if 0 <= step - 2 < GROUPS:
+                rotation_products(step - 2)

@@ -43,7 +43,8 @@ def tile_attention_pa_t_kernel(tc, x, wqk_w_words, wqk_w_scales, out_0, out_1):
         const = ctx.enter_context(tc.tile_pool(name="const", bufs=1))
         x_pool = ctx.enter_context(tc.tile_pool(name="x_pool", bufs=1))
         quant = ctx.enter_context(tc.tile_pool(name="quant", bufs=2))
-        rope = ctx.enter_context(tc.tile_pool(name="rope", bufs=4))
+        rope = ctx.enter_context(tc.tile_pool(name="rope", bufs=2))
+        result = ctx.enter_context(tc.tile_pool(name="result", bufs=1))
         xt_pool = ctx.enter_context(tc.psum_pool(name="xt_pool", bufs=6))
         acc_pool = ctx.enter_context(tc.psum_pool(name="acc_pool", bufs=2))
 
@@ -51,16 +52,22 @@ def tile_attention_pa_t_kernel(tc, x, wqk_w_words, wqk_w_scales, out_0, out_1):
         for g in range(GROUPS):
             x_rows.append(x_pool.tile([P, GROUP, FEATURES], BF16, name="x_rows_%d" % g))
 
-        def load_x(g):
+        def load_x(g, pieces):
             b, chunk = divmod(g, GROUPS_PER_BATCH)
             rows = x[b].rearrange("(p m) k -> p m k", m=ROWS)
-            nc.sync.dma_start(out=x_rows[g][:], in_=rows[:, GROUP * chunk : GROUP * (chunk + 1), :])
+            size = GROUP // pieces
+            for first in range(0, GROUP, size):
+                nc.sync.dma_start(
+                    out=x_rows[g][:, first : first + size, :],
+                    in_=rows[:, GROUP * chunk + first : GROUP * chunk + first + size, :],
+                )
 
         w_words = const.tile([P, PASSES, 2 * OUT_COLS], U8, align_bytes=64)
         w_scales = const.tile([P, PASSES, OUT_COLS], U8, align_bytes=64)
         nc.vector.memset(w_scales[:].bitcast(I32), 0)
 
-        load_x(0)
+        load_x(0, pieces=GROUP)
+        load_x(1, pieces=1)
         nc.sync.dma_start(
             out=w_words[:].bitcast(I32), in_=wqk_w_words.bitcast(I32).rearrange("c p n -> p c n")
         )
@@ -70,8 +77,8 @@ def tile_attention_pa_t_kernel(tc, x, wqk_w_words, wqk_w_scales, out_0, out_1):
                 out=w_scales[32 * quadrant : 32 * quadrant + 4].bitcast(I32),
                 in_=scale_rows[:, 4 * quadrant : 4 * quadrant + 4, :].rearrange("c r n -> r c n"),
             )
-        for g in range(1, GROUPS):
-            load_x(g)
+        for g in range(2, GROUPS):
+            load_x(g, pieces=1)
 
         position_int = const.tile([P, ROWS], I32)
         nc.gpsimd.iota(position_int[:], pattern=[[1, ROWS]], base=0, channel_multiplier=ROWS)
@@ -175,7 +182,7 @@ def tile_attention_pa_t_kernel(tc, x, wqk_w_words, wqk_w_scales, out_0, out_1):
             tiles = slice(GROUP * chunk, GROUP * (chunk + 1))
             acc = acc_of[g]
             pairs = acc[:].rearrange("p j (h i e) -> p j h i e", h=2, e=2)
-            rotated = rope.tile([P, 2, GROUP, HEAD], F32)
+            rotated = result.tile([P, 2, GROUP, HEAD], F32, name="rotated_%d" % g)
             cross = rope.tile([P, 2, 2, GROUP, PAIRS], F32)
             rotated_of[g] = (rotated, cross)
             nc.vector.tensor_tensor(

@@ -65,6 +65,9 @@ def tile_attention_pa_t_kernel(tc, x, wqk_w_words, wqk_w_scales, out_0, out_1):
         w_words = const.tile([P, PASSES, 2 * OUT_COLS], U8, align_bytes=64)
         w_scales = const.tile([P, PASSES, OUT_COLS], U8, align_bytes=64)
         nc.vector.memset(w_scales[:].bitcast(I32), 0)
+        warm = const.tile([P, 1], F32)
+        nc.vector.memset(warm[:], 0.0)
+        nc.scalar.activation(out=warm[:], in_=warm[:], func=ACT.Sin)
 
         load_x(0, pieces=GROUP)
         load_x(1, pieces=1)
@@ -113,20 +116,26 @@ def tile_attention_pa_t_kernel(tc, x, wqk_w_words, wqk_w_scales, out_0, out_1):
             out=part_turns[:], in0=turns[:], in1=whole_turns[:], op=ALU.subtract
         )
         sin_cos = const.tile([P, 2, ROWS, PAIRS], F32)
-        nc.scalar.activation(out=sin_cos[:], in_=part_turns[:], func=ACT.Sin, scale=2.0 * math.pi)
         sin = sin_cos[:, 0]
         neg_sin = const.tile([P, ROWS, PAIRS], F32)
-        nc.vector.tensor_scalar(
-            out=neg_sin[:], in0=sin, scalar1=-1.0, scalar2=None, op0=ALU.mult
-        )
         cos_twice = const.tile([P, ROWS, HEAD], F32)
-        nc.vector.tensor_copy(
-            out=cos_twice[:].rearrange("p m (i e) -> p (m i) e", e=2),
-            in_=sin_cos[:, 1]
-            .rearrange("p m i -> p (m i)")
-            .unsqueeze(2)
-            .to_broadcast([P, ROWS * PAIRS, 2]),
-        )
+
+        def sine_and_cosine():
+            nc.scalar.activation(
+                out=sin_cos[:], in_=part_turns[:], func=ACT.Sin, scale=2.0 * math.pi
+            )
+
+        def rotation_tables():
+            nc.vector.tensor_scalar(
+                out=neg_sin[:], in0=sin, scalar1=-1.0, scalar2=None, op0=ALU.mult
+            )
+            nc.vector.tensor_copy(
+                out=cos_twice[:].rearrange("p m (i e) -> p (m i) e", e=2),
+                in_=sin_cos[:, 1]
+                .rearrange("p m i -> p (m i)")
+                .unsqueeze(2)
+                .to_broadcast([P, ROWS * PAIRS, 2]),
+            )
 
         grouped_of = {}
         codes_of = {}
@@ -155,11 +164,12 @@ def tile_attention_pa_t_kernel(tc, x, wqk_w_words, wqk_w_scales, out_0, out_1):
             codes = quant.tile([P, GROUP, PASSES, P], U32, align_bytes=64)
             scales = quant.tile([P, GROUP, PASSES, P], U8, align_bytes=64)
             codes_of[g] = (codes, scales)
-            nc.vector.quantize_mx(
-                out=codes[:].rearrange("p j c r -> p (j c r)").bitcast(FP8X4),
-                scales=scales[:].rearrange("p j c r -> p (j c r)"),
-                in_=grouped_of[g][:].rearrange("p j c r t -> p (j c r t)"),
-            )
+            for j in range(GROUP):
+                nc.vector.quantize_mx(
+                    out=codes[:, j].rearrange("p c r -> p (c r)").bitcast(FP8X4),
+                    scales=scales[:, j].rearrange("p c r -> p (c r)"),
+                    in_=grouped_of[g][:, j].rearrange("p c r t -> p (c r t)"),
+                )
 
         def multiply_group(g):
             codes, scales = codes_of[g]
@@ -209,7 +219,7 @@ def tile_attention_pa_t_kernel(tc, x, wqk_w_words, wqk_w_scales, out_0, out_1):
             tiles = slice(GROUP * chunk, GROUP * (chunk + 1))
             rotated, cross = rotated_of[g]
             by_pair = rotated[:].rearrange("p h j (i e) -> p (h j i) e", e=2)
-            nc.vector.tensor_tensor(
+            nc.gpsimd.tensor_tensor(
                 out=by_pair,
                 in0=by_pair,
                 in1=cross[:].rearrange("p e h j i -> p (h j i) e"),
@@ -219,13 +229,16 @@ def tile_attention_pa_t_kernel(tc, x, wqk_w_words, wqk_w_scales, out_0, out_1):
                 rows = out[b, 0].rearrange("(p m) f -> p m f", m=ROWS)
                 nc.sync.dma_start(out=rows[:, tiles, :], in_=rotated[:, h])
 
-        for step in range(GROUPS + 3):
+        for step in range(GROUPS + 2):
             if step < GROUPS:
                 transpose_group(step)
+            if step == 0:
+                sine_and_cosine()
             if 0 <= step - 1 < GROUPS:
                 quantise_group(step - 1)
                 multiply_group(step - 1)
-            if 0 <= step - 3 < GROUPS:
-                rotation_sum_and_store(step - 3)
+            if step == 1:
+                rotation_tables()
             if 0 <= step - 2 < GROUPS:
                 rotation_products(step - 2)
+                rotation_sum_and_store(step - 2)

@@ -219,7 +219,8 @@ def tile_attention_pa_t_kernel(tc, x, wqk_w_words, wqk_w_scales, out_0, out_1):
             tiles = slice(GROUP * chunk, GROUP * (chunk + 1))
             rotated, cross = rotated_of[g]
             by_pair = rotated[:].rearrange("p h j (i e) -> p (h j i) e", e=2)
-            nc.gpsimd.tensor_tensor(
+            adder = nc.vector if g == GROUPS - 1 else nc.gpsimd
+            adder.tensor_tensor(
                 out=by_pair,
                 in0=by_pair,
                 in1=cross[:].rearrange("p e h j i -> p (h j i) e"),

@@ -31,6 +31,9 @@ GROUP = 4
 GROUPS_PER_BATCH = ROWS // GROUP
 GROUPS = BATCH * GROUPS_PER_BATCH
 
+SORT_EVERY = 2
+FIRST_SORTED = 3
+
 ROUND_MAGIC = 12582912.0
 
 FLOPS = 2 * BATCH * SEQ * FEATURES * OUT_COLS
@@ -44,6 +47,7 @@ def tile_attention_pa_t_kernel(tc, x, wqk_w_words, wqk_w_scales, out_0, out_1):
         x_pool = ctx.enter_context(tc.tile_pool(name="x_pool", bufs=1))
         quant = ctx.enter_context(tc.tile_pool(name="quant", bufs=2))
         rope = ctx.enter_context(tc.tile_pool(name="rope", bufs=2))
+        sorted_pool = ctx.enter_context(tc.tile_pool(name="sorted_pool", bufs=2))
         result = ctx.enter_context(tc.tile_pool(name="result", bufs=1))
         xt_pool = ctx.enter_context(tc.psum_pool(name="xt_pool", bufs=6))
         acc_pool = ctx.enter_context(tc.psum_pool(name="acc_pool", bufs=2))
@@ -142,6 +146,19 @@ def tile_attention_pa_t_kernel(tc, x, wqk_w_words, wqk_w_scales, out_0, out_1):
         acc_of = {}
         rotated_of = {}
 
+        sorted_of = {}
+
+        def sorts_words(g):
+            return g >= FIRST_SORTED and g % SORT_EVERY == FIRST_SORTED % SORT_EVERY
+
+        def sort_words(g):
+            words = x_rows[g][:, GROUP - 1, :].bitcast(F32)
+            by_half = sorted_pool.tile([P, PASSES, 2, P], F32)
+            sorted_of[g] = by_half
+            nc.scalar.copy(
+                out=by_half[:], in_=words.rearrange("p (c w u) -> p c u w", c=PASSES, u=2)
+            )
+
         def transpose_group(g):
             grouped = quant.tile([P, GROUP, PASSES, P, PACK], BF16, align_bytes=64)
             grouped_of[g] = grouped
@@ -151,11 +168,11 @@ def tile_attention_pa_t_kernel(tc, x, wqk_w_words, wqk_w_scales, out_0, out_1):
                 for c in range(PASSES):
                     for u in range(2):
                         first = WORDS_PER_PASS * c + u
-                        nc.tensor.transpose(
-                            xt[:, c, u, :],
-                            words[:, first : WORDS_PER_PASS * (c + 1) : 2],
-                            ident[:],
-                        )
+                        if j == GROUP - 1 and sorts_words(g):
+                            every_second_word = sorted_of[g][:, c, u, :]
+                        else:
+                            every_second_word = words[:, first : WORDS_PER_PASS * (c + 1) : 2]
+                        nc.tensor.transpose(xt[:, c, u, :], every_second_word, ident[:])
                 nc.scalar.copy(
                     out=grouped[:, j].bitcast(F32), in_=xt[:].rearrange("p c u r -> p c r u")
                 )
@@ -233,6 +250,8 @@ def tile_attention_pa_t_kernel(tc, x, wqk_w_words, wqk_w_scales, out_0, out_1):
         for step in range(GROUPS + 2):
             if step < GROUPS:
                 transpose_group(step)
+            if step + 1 < GROUPS and sorts_words(step + 1):
+                sort_words(step + 1)
             if step == 0:
                 sine_and_cosine()
             if 0 <= step - 1 < GROUPS:

@@ -121,7 +121,7 @@ def tile_attention_pa_t_kernel(tc, x, wqk_w_words, wqk_w_scales, out_0, out_1):
         )
         sin_cos = const.tile([P, 2, ROWS, PAIRS], F32)
         sin = sin_cos[:, 0]
-        neg_sin = const.tile([P, ROWS, PAIRS], F32)
+        signed_sin = const.tile([P, ROWS, PAIRS, 2], F32)
         cos_twice = const.tile([P, ROWS, HEAD], F32)
 
         def sine_and_cosine():
@@ -131,8 +131,9 @@ def tile_attention_pa_t_kernel(tc, x, wqk_w_words, wqk_w_scales, out_0, out_1):
 
         def rotation_tables():
             nc.vector.tensor_scalar(
-                out=neg_sin[:], in0=sin, scalar1=-1.0, scalar2=None, op0=ALU.mult
+                out=signed_sin[:, :, :, 0], in0=sin, scalar1=-1.0, scalar2=None, op0=ALU.mult
             )
+            nc.vector.tensor_copy(out=signed_sin[:, :, :, 1], in_=sin)
             nc.vector.tensor_copy(
                 out=cos_twice[:].rearrange("p m (i e) -> p (m i) e", e=2),
                 in_=sin_cos[:, 1]
@@ -210,18 +211,12 @@ def tile_attention_pa_t_kernel(tc, x, wqk_w_words, wqk_w_scales, out_0, out_1):
             acc = acc_of[g]
             pairs = acc[:].rearrange("p j (h i e) -> p j h i e", h=2, e=2)
             rotated = result.tile([P, 2, GROUP, HEAD], F32, name="rotated_%d" % g)
-            cross = rope.tile([P, 2, 2, GROUP, PAIRS], F32)
+            cross = rope.tile([P, 2, GROUP, HEAD], F32)
             rotated_of[g] = (rotated, cross)
             nc.vector.tensor_tensor(
-                out=cross[:, 0].rearrange("p h j i -> p j h i"),
-                in0=pairs[:, :, :, :, 1],
-                in1=neg_sin[:, tiles, :].unsqueeze(2).to_broadcast([P, GROUP, 2, PAIRS]),
-                op=ALU.mult,
-            )
-            nc.vector.tensor_tensor(
-                out=cross[:, 1].rearrange("p h j i -> p j h i"),
-                in0=pairs[:, :, :, :, 0],
-                in1=sin[:, tiles, :].unsqueeze(2).to_broadcast([P, GROUP, 2, PAIRS]),
+                out=cross[:].rearrange("p h j (i e) -> p j h i e", e=2),
+                in0=pairs[:, :, :, :, ::-1],
+                in1=signed_sin[:, tiles].unsqueeze(2).to_broadcast([P, GROUP, 2, PAIRS, 2]),
                 op=ALU.mult,
             )
             nc.vector.tensor_tensor(
@@ -235,12 +230,12 @@ def tile_attention_pa_t_kernel(tc, x, wqk_w_words, wqk_w_scales, out_0, out_1):
             b, chunk = divmod(g, GROUPS_PER_BATCH)
             tiles = slice(GROUP * chunk, GROUP * (chunk + 1))
             rotated, cross = rotated_of[g]
-            by_pair = rotated[:].rearrange("p h j (i e) -> p (h j i) e", e=2)
+            flat = rotated[:].rearrange("p h j f -> p (h j f)")
             adder = nc.vector if g == GROUPS - 1 else nc.gpsimd
             adder.tensor_tensor(
-                out=by_pair,
-                in0=by_pair,
-                in1=cross[:].rearrange("p e h j i -> p (h j i) e"),
+                out=flat,
+                in0=flat,
+                in1=cross[:].rearrange("p h j f -> p (h j f)"),
                 op=ALU.add,
             )
             for h, out in enumerate((out_0, out_1)):

@@ -32,7 +32,7 @@ GROUPS_PER_BATCH = ROWS // GROUP
 GROUPS = BATCH * GROUPS_PER_BATCH
 
 SORT_EVERY = 2
-FIRST_SORTED = 3
+FIRST_SORTED = 2
 
 ROUND_MAGIC = 12582912.0
 

import math
from contextlib import ExitStack

import concourse.mybir as mybir
from concourse.masks import make_identity

F32 = mybir.dt.float32
BF16 = mybir.dt.bfloat16
I32 = mybir.dt.int32
U32 = mybir.dt.uint32
U8 = mybir.dt.uint8
FP8X4 = mybir.dt.float8_e4m3fn_x4
FP4X4 = mybir.dt.float4_e2m1fn_x4
ALU = mybir.AluOpType
ACT = mybir.ActivationFunctionType

BATCH, SEQ, FEATURES = 4, 2048, 1024
HEAD = 64
PAIRS = HEAD // 2
OUT_COLS = 2 * HEAD
ROPE_BASE = 10000.0

P = 128
PACK = 4
K_PASS = P * PACK
PASSES = FEATURES // K_PASS
WORDS_PER_PASS = K_PASS // 2

ROWS = SEQ // P
GROUP = 4
GROUPS_PER_BATCH = ROWS // GROUP
GROUPS = BATCH * GROUPS_PER_BATCH

SORT_EVERY = 2
FIRST_SORTED = 2

ROUND_MAGIC = 12582912.0

FLOPS = 2 * BATCH * SEQ * FEATURES * OUT_COLS


def tile_attention_pa_t_kernel(tc, x, wqk_w_words, wqk_w_scales, out_0, out_1):
    nc = tc.nc
    with ExitStack() as ctx:
        ctx.enter_context(tc.manual_schedule())
        const = ctx.enter_context(tc.tile_pool(name="const", bufs=1))
        x_pool = ctx.enter_context(tc.tile_pool(name="x_pool", bufs=1))
        quant = ctx.enter_context(tc.tile_pool(name="quant", bufs=2))
        rope = ctx.enter_context(tc.tile_pool(name="rope", bufs=2))
        sorted_pool = ctx.enter_context(tc.tile_pool(name="sorted_pool", bufs=2))
        result = ctx.enter_context(tc.tile_pool(name="result", bufs=1))
        xt_pool = ctx.enter_context(tc.psum_pool(name="xt_pool", bufs=6))
        acc_pool = ctx.enter_context(tc.psum_pool(name="acc_pool", bufs=2))

        x_rows = []
        for g in range(GROUPS):
            x_rows.append(x_pool.tile([P, GROUP, FEATURES], BF16, name="x_rows_%d" % g))

        def load_x(g, pieces):
            b, chunk = divmod(g, GROUPS_PER_BATCH)
            rows = x[b].rearrange("(p m) k -> p m k", m=ROWS)
            size = GROUP // pieces
            for first in range(0, GROUP, size):
                nc.sync.dma_start(
                    out=x_rows[g][:, first : first + size, :],
                    in_=rows[:, GROUP * chunk + first : GROUP * chunk + first + size, :],
                )

        w_words = const.tile([P, PASSES, 2 * OUT_COLS], U8, align_bytes=64)
        w_scales = const.tile([P, PASSES, OUT_COLS], U8, align_bytes=64)
        nc.vector.memset(w_scales[:].bitcast(I32), 0)
        warm = const.tile([P, 1], F32)
        nc.vector.memset(warm[:], 0.0)
        nc.scalar.activation(out=warm[:], in_=warm[:], func=ACT.Sin)

        load_x(0, pieces=GROUP)
        load_x(1, pieces=1)
        nc.sync.dma_start(
            out=w_words[:].bitcast(I32), in_=wqk_w_words.bitcast(I32).rearrange("c p n -> p c n")
        )
        scale_rows = wqk_w_scales.bitcast(I32)
        for quadrant in range(4):
            nc.sync.dma_start(
                out=w_scales[32 * quadrant : 32 * quadrant + 4].bitcast(I32),
                in_=scale_rows[:, 4 * quadrant : 4 * quadrant + 4, :].rearrange("c r n -> r c n"),
            )
        for g in range(2, GROUPS):
            load_x(g, pieces=1)

        position_int = const.tile([P, ROWS], I32)
        nc.gpsimd.iota(position_int[:], pattern=[[1, ROWS]], base=0, channel_multiplier=ROWS)
        ident = const.tile([P, P], F32)
        make_identity(nc, ident[:])
        position = const.tile([P, ROWS], F32)
        nc.vector.tensor_copy(out=position[:], in_=position_int[:])
        turns = const.tile([P, 2, ROWS, PAIRS], F32)
        for i in range(PAIRS):
            turns_per_position = ROPE_BASE ** (-2.0 * i / HEAD) / (2.0 * math.pi)
            nc.vector.tensor_scalar(
                out=turns[:, 0, :, i],
                in0=position[:],
                scalar1=turns_per_position,
                scalar2=None,
                op0=ALU.mult,
            )
        nc.vector.tensor_scalar(
            out=turns[:, 1], in0=turns[:, 0], scalar1=0.25, scalar2=None, op0=ALU.add
        )
        whole_turns = const.tile([P, 2, ROWS, PAIRS], F32)
        nc.vector.tensor_scalar(
            out=whole_turns[:],
            in0=turns[:],
            scalar1=ROUND_MAGIC,
            scalar2=ROUND_MAGIC,
            op0=ALU.add,
            op1=ALU.subtract,
        )
        part_turns = const.tile([P, 2, ROWS, PAIRS], F32)
        nc.vector.tensor_tensor(
            out=part_turns[:], in0=turns[:], in1=whole_turns[:], op=ALU.subtract
        )
        sin_cos = const.tile([P, 2, ROWS, PAIRS], F32)
        sin = sin_cos[:, 0]
        signed_sin = const.tile([P, ROWS, PAIRS, 2], F32)
        cos_twice = const.tile([P, ROWS, HEAD], F32)

        def sine_and_cosine():
            nc.scalar.activation(
                out=sin_cos[:], in_=part_turns[:], func=ACT.Sin, scale=2.0 * math.pi
            )

        def rotation_tables():
            nc.vector.tensor_scalar(
                out=signed_sin[:, :, :, 0], in0=sin, scalar1=-1.0, scalar2=None, op0=ALU.mult
            )
            nc.vector.tensor_copy(out=signed_sin[:, :, :, 1], in_=sin)
            nc.vector.tensor_copy(
                out=cos_twice[:].rearrange("p m (i e) -> p (m i) e", e=2),
                in_=sin_cos[:, 1]
                .rearrange("p m i -> p (m i)")
                .unsqueeze(2)
                .to_broadcast([P, ROWS * PAIRS, 2]),
            )

        grouped_of = {}
        codes_of = {}
        acc_of = {}
        rotated_of = {}

        sorted_of = {}

        def sorts_words(g):
            return g >= FIRST_SORTED and g % SORT_EVERY == FIRST_SORTED % SORT_EVERY

        def sort_words(g):
            words = x_rows[g][:, GROUP - 1, :].bitcast(F32)
            by_half = sorted_pool.tile([P, PASSES, 2, P], F32)
            sorted_of[g] = by_half
            nc.scalar.copy(
                out=by_half[:], in_=words.rearrange("p (c w u) -> p c u w", c=PASSES, u=2)
            )

        def transpose_group(g):
            grouped = quant.tile([P, GROUP, PASSES, P, PACK], BF16, align_bytes=64)
            grouped_of[g] = grouped
            for j in range(GROUP):
                words = x_rows[g][:, j, :].bitcast(F32)
                xt = xt_pool.tile([P, PASSES, 2, P], F32)
                for c in range(PASSES):
                    for u in range(2):
                        first = WORDS_PER_PASS * c + u
                        if j == GROUP - 1 and sorts_words(g):
                            every_second_word = sorted_of[g][:, c, u, :]
                        else:
                            every_second_word = words[:, first : WORDS_PER_PASS * (c + 1) : 2]
                        nc.tensor.transpose(xt[:, c, u, :], every_second_word, ident[:])
                nc.scalar.copy(
                    out=grouped[:, j].bitcast(F32), in_=xt[:].rearrange("p c u r -> p c r u")
                )

        def quantise_group(g):
            codes = quant.tile([P, GROUP, PASSES, P], U32, align_bytes=64)
            scales = quant.tile([P, GROUP, PASSES, P], U8, align_bytes=64)
            codes_of[g] = (codes, scales)
            for j in range(GROUP):
                nc.vector.quantize_mx(
                    out=codes[:, j].rearrange("p c r -> p (c r)").bitcast(FP8X4),
                    scales=scales[:, j].rearrange("p c r -> p (c r)"),
                    in_=grouped_of[g][:, j].rearrange("p c r t -> p (c r t)"),
                )

        def multiply_group(g):
            codes, scales = codes_of[g]
            acc = acc_pool.tile([P, GROUP, OUT_COLS], F32)
            acc_of[g] = acc
            for j in range(GROUP):
                for c in range(PASSES):
                    nc.tensor.matmul_mx(
                        out=acc[:, j, :],
                        lhsT=codes[:, j, c, :].bitcast(FP8X4),
                        lhsT_scale=scales[:, j, c, :],
                        rhs=w_words[:, c, :].bitcast(FP4X4),
                        rhs_scale=w_scales[:, c, :],
                        start=(c == 0),
                        stop=(c == PASSES - 1),
                    )

        def rotation_products(g):
            chunk = g % GROUPS_PER_BATCH
            tiles = slice(GROUP * chunk, GROUP * (chunk + 1))
            acc = acc_of[g]
            pairs = acc[:].rearrange("p j (h i e) -> p j h i e", h=2, e=2)
            rotated = result.tile([P, 2, GROUP, HEAD], F32, name="rotated_%d" % g)
            cross = rope.tile([P, 2, GROUP, HEAD], F32)
            rotated_of[g] = (rotated, cross)
            nc.vector.tensor_tensor(
                out=cross[:].rearrange("p h j (i e) -> p j h i e", e=2),
                in0=pairs[:, :, :, :, ::-1],
                in1=signed_sin[:, tiles].unsqueeze(2).to_broadcast([P, GROUP, 2, PAIRS, 2]),
                op=ALU.mult,
            )
            nc.vector.tensor_tensor(
                out=rotated[:].rearrange("p h j f -> p j h f"),
                in0=acc[:].rearrange("p j (h f) -> p j h f", h=2),
                in1=cos_twice[:, tiles, :].unsqueeze(2).to_broadcast([P, GROUP, 2, HEAD]),
                op=ALU.mult,
            )

        def rotation_sum_and_store(g):
            b, chunk = divmod(g, GROUPS_PER_BATCH)
            tiles = slice(GROUP * chunk, GROUP * (chunk + 1))
            rotated, cross = rotated_of[g]
            flat = rotated[:].rearrange("p h j f -> p (h j f)")
            adder = nc.vector if g == GROUPS - 1 else nc.gpsimd
            adder.tensor_tensor(
                out=flat,
                in0=flat,
                in1=cross[:].rearrange("p h j f -> p (h j f)"),
                op=ALU.add,
            )
            for h, out in enumerate((out_0, out_1)):
                rows = out[b, 0].rearrange("(p m) f -> p m f", m=ROWS)
                nc.sync.dma_start(out=rows[:, tiles, :], in_=rotated[:, h])

        for step in range(GROUPS + 2):
            if step < GROUPS:
                transpose_group(step)
            if step + 1 < GROUPS and sorts_words(step + 1):
                sort_words(step + 1)
            if step == 0:
                sine_and_cosine()
            if 0 <= step - 1 < GROUPS:
                quantise_group(step - 1)
                multiply_group(step - 1)
            if step == 1:
                rotation_tables()
            if 0 <= step - 2 < GROUPS:
                rotation_products(step - 2)
                rotation_sum_and_store(step - 2)
